import numpy as np
import ml_dtypes


def mxq(x, axis, fmt="e4m3"):
    dtype, down = {"e4m3": (ml_dtypes.float8_e4m3fn, 7), "e5m2": (ml_dtypes.float8_e5m2, 14)}[fmt]
    v = np.moveaxis(np.asarray(x, np.float32).astype(ml_dtypes.bfloat16).astype(np.float64), axis, -1)
    blocks = v.reshape(v.shape[:-1] + (-1, 32))
    amax = np.abs(blocks).max(-1, keepdims=True)
    byte = np.maximum(np.where(amax > 0, np.frexp(amax)[1] - 1 + 127, 0) - down, 1)
    scale = np.exp2(byte - 127.0)
    codes = (blocks / scale).astype(np.float32).astype(dtype).astype(np.float64)
    return np.moveaxis((codes * scale).reshape(v.shape), -1, axis)


WIDE = False


def mx_kscale(k):
    if not WIDE:
        return np.ones(k)
    levels = np.array([10, -10, 5, -5, 0])
    a = np.random.permutation(np.resize(levels, k // 512 * 4)).reshape(k // 512, 4)
    idx = np.arange(k)
    return np.exp2(a[idx // 512, idx % 128 // 32])


BF16 = ml_dtypes.bfloat16


def bf(x):
    return np.asarray(x, np.float32).astype(BF16)


def f64(x):
    return np.asarray(x).astype(np.float64)


B, S, H, F = 128, 8, 512, 512


def setup_inputs():
    s = mx_kscale(H)
    t = mx_kscale(F)
    s2 = np.concatenate([s, s])
    return {"h": bf(np.random.standard_normal((B, S, H)) * s),
            "ew1": bf(np.random.standard_normal((2 * H, F)) / np.sqrt(2 * H) / s2[:, None] * t),
            "eb1": bf(np.random.standard_normal(F) * 0.3 * t),
            "ew2": bf(np.random.standard_normal((F, H)) / np.sqrt(F) / t[:, None]),
            "eb2": bf(np.random.standard_normal(H) * 0.3)}


def edge_mlp(xq, w1q, b1, w2q, b2):
    hid = np.maximum((xq @ w1q) + b1, 0.0)
    return (mxq(hid, 2, "e4m3") @ w2q) + b2


def reference(h, ew1, eb1, ew2, eb2):
    hq = mxq(f64(h), 2, "e4m3")
    w1q = mxq(f64(ew1), 0, "e4m3")
    w2q = mxq(f64(ew2), 0, "e4m3")
    b1, b2 = f64(eb1), f64(eb2)
    left = hq[:, :-1, :]
    right = hq[:, 1:, :]
    m_lr = edge_mlp(np.concatenate([left, right], axis=-1), w1q, b1, w2q, b2)
    m_rl = edge_mlp(np.concatenate([right, left], axis=-1), w1q, b1, w2q, b2)
    zcol = np.zeros_like(m_lr[:, :1, :])
    return np.concatenate([zcol, m_lr], axis=1) + np.concatenate([m_rl, zcol], axis=1)

@@ -1,0 +1,263 @@
+from contextlib import ExitStack
+
+import concourse.mybir as mybir
+from concourse.masks import make_identity
+
+BF16 = mybir.dt.bfloat16
+F32 = mybir.dt.float32
+U32 = mybir.dt.uint32
+U8 = mybir.dt.uint8
+FP8X4 = mybir.dt.float8_e4m3fn_x4
+RELU = mybir.ActivationFunctionType.Relu
+ADD = mybir.AluOpType.add
+MULT = mybir.AluOpType.mult
+
+P = 128
+PACK = 4
+NODES = 8
+EDGES = NODES - 1
+H = 512
+F = 512
+PART_NODES = 4
+UNIT_EDGES = 2
+UNIT_TOKENS = UNIT_EDGES * P
+LAG = 2
+RUN = 4
+VECTOR_COLS = 352
+
+FLOPS = 2 * 2 * EDGES * P * (2 * H * F + F * H)
+
+
+def edge_units():
+    units = []
+    for first in range(0, EDGES - 1, UNIT_EDGES):
+        units.append([("rl", first, UNIT_EDGES)])
+        units.append([("lr", first, UNIT_EDGES)])
+    units.append([("rl", EDGES - 1, 1), ("lr", EDGES - 1, 1)])
+    return units
+
+
+def tile_graphnetlayer_pa_kernel(tc, h, ew1, eb1, ew2, eb2, out):
+    nc = tc.nc
+    units = edge_units()
+
+    with ExitStack() as ctx:
+        ctx.enter_context(tc.manual_schedule())
+        keep = ctx.enter_context(tc.tile_pool(name="keep", bufs=1))
+        stream = ctx.enter_context(tc.tile_pool(name="stream", bufs=LAG + 2))
+        psum_hidden = ctx.enter_context(tc.psum_pool(name="psum_hidden", bufs=4))
+        psum_node = ctx.enter_context(tc.psum_pool(name="psum_node", bufs=4))
+
+        b1_rows = keep.tile([P, P], BF16, name="b1_rows")
+        b2_rows = keep.tile([P, H], BF16, name="b2_rows")
+        ones = keep.tile([P, P], BF16, name="ones")
+        nc.vector.memset(b1_rows[:], 0.0)
+        nc.vector.memset(b2_rows[:], 0.0)
+        nc.vector.memset(ones[:], 1.0)
+        w1_raw = keep.tile([P, 2, PACK, F], BF16, name="w1_raw")
+        h_raw = keep.tile([P, NODES * H], BF16, name="h_raw")
+        w2_raw = keep.tile([P, PACK, H], BF16, name="w2_raw")
+        h_flat = h.rearrange("b s k -> b (s k)")
+
+        def load_w1(half):
+            nc.sync.dma_start(
+                out=w1_raw[:, half].rearrange("p (u e) c -> p u e c", e=2),
+                in_=ew1[half * H : (half + 1) * H, :].rearrange("(u p e) c -> p u e c", u=2, e=2),
+            )
+
+        def load_h(part):
+            cols = slice(part * PART_NODES * H, (part + 1) * PART_NODES * H)
+            nc.sync.dma_start(out=h_raw[:, cols], in_=h_flat[:, cols])
+
+        load_w1(0)
+        nc.sync.dma_start(out=b1_rows[0:PACK, :], in_=eb1.rearrange("(t p) -> t p", p=P))
+        nc.sync.dma_start(out=b2_rows[0:1, :], in_=eb2.rearrange("(o n) -> o n", o=1))
+        load_h(0)
+        load_w1(1)
+        load_h(1)
+        nc.sync.dma_start(out=w2_raw[:], in_=ew2.rearrange("(t p) n -> p t n", p=P))
+
+        ident_f32 = keep.tile([P, P], F32, name="ident_f32")
+        ident_bf16 = keep.tile([P, P], BF16, name="ident_bf16")
+        make_identity(nc, ident_f32[:])
+        nc.vector.tensor_copy(out=ident_bf16[:], in_=ident_f32[:])
+
+        def regroup_weight(raw, grouped):
+            src = raw.rearrange("p t (c i) -> p c t i", i=RUN)
+            dst = grouped.rearrange("p (c i) t -> p c t i", i=RUN)
+            split = VECTOR_COLS // RUN
+            nc.vector.tensor_copy(out=dst[:, :split], in_=src[:, :split])
+            nc.scalar.copy(out=dst[:, split:], in_=src[:, split:])
+
+        def quantise(grouped, codes, scales):
+            nc.vector.quantize_mx(
+                out=codes.bitcast(FP8X4),
+                scales=scales,
+                in_=grouped.rearrange("p c t -> p (c t)"),
+            )
+
+        w1_grouped = keep.tile([P, 2, F, PACK], BF16, name="w1_grouped", align_bytes=64)
+        w1_codes = keep.tile([P, 2, F], U32, name="w1_codes", align_bytes=64)
+        w1_scales = keep.tile([P, 2, F], U8, name="w1_scales", align_bytes=64)
+
+        h_words = h_raw[:].bitcast(F32)
+        h_grouped = keep.tile([P, NODES, P, PACK], BF16, name="h_grouped", align_bytes=64)
+        h_grouped_words = h_grouped[:].rearrange("p s b t -> p (s b t)").bitcast(F32)
+        h_codes = keep.tile([P, NODES * P], U32, name="h_codes", align_bytes=64)
+        h_scales = keep.tile([P, NODES * P], U8, name="h_scales", align_bytes=64)
+        words = H // 2
+
+        def flip_h(part):
+            for pair in range(part * PART_NODES // 2, (part + 1) * PART_NODES // 2):
+                flipped = psum_hidden.tile([P, 2, 2, P], F32, name="flipped", tag="hidden_acc")
+                for s in range(2):
+                    for u in range(2):
+                        first = (2 * pair + s) * words + u * P
+                        nc.tensor.transpose(
+                            flipped[:, s, u, :], h_words[:, first : first + P], ident_f32[:]
+                        )
+                nc.scalar.copy(
+                    out=h_grouped_words[:, 2 * pair * words : (2 * pair + 2) * words].rearrange(
+                        "p (s b u) -> p s b u", s=2, u=2
+                    ),
+                    in_=flipped[:].rearrange("p s u b -> p s b u"),
+                )
+
+        def quantise_h(part):
+            nodes = slice(part * PART_NODES, (part + 1) * PART_NODES)
+            tokens = slice(part * PART_NODES * P, (part + 1) * PART_NODES * P)
+            quantise(
+                h_grouped[:, nodes].rearrange("p s b t -> p (s b) t"),
+                h_codes[:, tokens],
+                h_scales[:, tokens],
+            )
+
+        regroup_weight(w1_raw[:, 0], w1_grouped[:, 0])
+        b1_t = psum_node.tile([P, P], BF16, name="b1_t", tag="node_acc")
+        nc.tensor.transpose(b1_t[:], b1_rows[:], ident_bf16[:])
+        b1_col = keep.tile([P, PACK], F32, name="b1_col")
+        nc.vector.tensor_copy(out=b1_col[:], in_=b1_t[:, 0:PACK])
+        quantise(w1_grouped[:, 0], w1_codes[:, 0], w1_scales[:, 0])
+        flip_h(0)
+        regroup_weight(w1_raw[:, 1], w1_grouped[:, 1])
+        quantise_h(0)
+        quantise(w1_grouped[:, 1], w1_codes[:, 1], w1_scales[:, 1])
+        flip_h(1)
+        quantise_h(1)
+
+        hidden_of = {}
+        grouped_of = {}
+        codes_of = {}
+        node_acc = {}
+        terms_seen = {}
+        out_sb = keep.tile([P, NODES, H], F32, name="out_sb")
+
+        def layer1(u):
+            hidden = stream.tile([P, PACK, UNIT_TOKENS], BF16, name="hidden")
+            hidden_of[u] = hidden
+            for bank in range(PACK // 2):
+                acc = psum_hidden.tile([P, 2, UNIT_TOKENS], F32, name="hidden_acc")
+                for i in range(2):
+                    f_cols = slice((2 * bank + i) * P, (2 * bank + i + 1) * P)
+                    col = 0
+                    for direction, first_edge, edges in units[u]:
+                        width = edges * P
+                        left = slice(first_edge * P, first_edge * P + width)
+                        right = slice((first_edge + 1) * P, (first_edge + 1) * P + width)
+                        joined = (left, right) if direction == "lr" else (right, left)
+                        for half in range(2):
+                            nc.tensor.matmul_mx(
+                                out=acc[:, i, col : col + width],
+                                lhsT=w1_codes[:, half, f_cols].bitcast(FP8X4),
+                                lhsT_scale=w1_scales[:, half, f_cols],
+                                rhs=h_codes[:, joined[half]].bitcast(FP8X4),
+                                rhs_scale=h_scales[:, joined[half]],
+                                start=(half == 0),
+                                stop=(half == 1),
+                            )
+                        col += width
+                for i in range(2):
+                    t = 2 * bank + i
+                    nc.scalar.activation(
+                        out=hidden[:, t, :],
+                        in_=acc[:, i, :],
+                        func=RELU,
+                        bias=b1_col[:, t : t + 1],
+                        scale=1.0,
+                    )
+
+        def regroup_hidden(u):
+            grouped = stream.tile([P, UNIT_TOKENS, PACK], BF16, name="grouped", align_bytes=64)
+            grouped_of[u] = grouped
+            nc.vector.tensor_copy(
+                out=grouped.rearrange("p (c i) t -> p c t i", i=RUN),
+                in_=hidden_of[u].rearrange("p t (c i) -> p c t i", i=RUN),
+            )
+
+        def quantise_hidden(u):
+            codes = stream.tile([P, UNIT_TOKENS], U32, name="codes", align_bytes=64)
+            scales = stream.tile([P, UNIT_TOKENS], U8, name="scales", align_bytes=64)
+            codes_of[u] = (codes, scales)
+            quantise(grouped_of[u], codes[:], scales[:])
+
+        def layer2(u):
+            codes, scales = codes_of[u]
+            finished = []
+            block = 0
+            for direction, first_edge, edges in units[u]:
+                for edge in range(first_edge, first_edge + edges):
+                    node = edge + 1 if direction == "lr" else edge
+                    terms = 1 if node in (0, NODES - 1) else 2
+                    if node not in node_acc:
+                        acc = psum_node.tile([P, H], F32, name="node_acc")
+                        node_acc[node] = acc
+                        terms_seen[node] = 0
+                    terms_seen[node] += 1
+                    tokens = slice(block * P, (block + 1) * P)
+                    nc.tensor.matmul_mx(
+                        out=node_acc[node][:],
+                        lhsT=codes[:, tokens].bitcast(FP8X4),
+                        lhsT_scale=scales[:, tokens],
+                        rhs=w2_codes[:].bitcast(FP8X4),
+                        rhs_scale=w2_scales[:],
+                        start=(terms_seen[node] == 1),
+                        stop=(terms_seen[node] == terms),
+                    )
+                    if terms_seen[node] == terms:
+                        finished.append(node)
+                    block += 1
+            return finished
+
+        def finish(nodes):
+            for node in nodes:
+                nc.vector.scalar_tensor_tensor(
+                    out=out_sb[:, node, :],
+                    in0=b2_all[:],
+                    scalar=float(terms_seen[node]),
+                    in1=node_acc[node][:],
+                    op0=MULT,
+                    op1=ADD,
+                )
+                nc.sync.dma_start(out=out[:, node, :], in_=out_sb[:, node, :])
+
+        layer1(0)
+        b2_sum = psum_node.tile([P, H], F32, name="b2_sum", tag="node_acc")
+        nc.tensor.matmul(b2_sum[:], lhsT=ones[:], rhs=b2_rows[:], start=True, stop=True)
+        b2_all = keep.tile([P, H], F32, name="b2_all")
+        nc.scalar.copy(out=b2_all[:], in_=b2_sum[:])
+        w2_grouped = keep.tile([P, H, PACK], BF16, name="w2_grouped", align_bytes=64)
+        w2_codes = keep.tile([P, H], U32, name="w2_codes", align_bytes=64)
+        w2_scales = keep.tile([P, H], U8, name="w2_scales", align_bytes=64)
+        regroup_weight(w2_raw[:], w2_grouped[:])
+        regroup_hidden(0)
+        quantise(w2_grouped[:], w2_codes[:], w2_scales[:])
+        quantise_hidden(0)
+        for u in range(1, len(units) + LAG):
+            if u < len(units):
+                layer1(u)
+            finished = layer2(u - LAG) if u >= LAG else []
+            if u < len(units):
+                regroup_hidden(u)
+            finish(finished)
+            if u < len(units):
+                quantise_hidden(u)

@@ -21,7 +21,8 @@ F = 512
 PART_NODES = 4
 UNIT_EDGES = 2
 UNIT_TOKENS = UNIT_EDGES * P
-LAG = 2
+BANK_F = 2 * P
+LAG = 3
 RUN = 4
 VECTOR_COLS = 352
 
@@ -49,14 +50,11 @@ def tile_graphnetlayer_pa_kernel(tc, h, ew1, eb1, ew2, eb2, out):
         psum_node = ctx.enter_context(tc.psum_pool(name="psum_node", bufs=4))
 
         b1_rows = keep.tile([P, P], BF16, name="b1_rows")
-        b2_rows = keep.tile([P, H], BF16, name="b2_rows")
-        ones = keep.tile([P, P], BF16, name="ones")
         nc.vector.memset(b1_rows[:], 0.0)
-        nc.vector.memset(b2_rows[:], 0.0)
-        nc.vector.memset(ones[:], 1.0)
         w1_raw = keep.tile([P, 2, PACK, F], BF16, name="w1_raw")
         h_raw = keep.tile([P, NODES * H], BF16, name="h_raw")
         w2_raw = keep.tile([P, PACK, H], BF16, name="w2_raw")
+        b2_all = keep.tile([P, H], BF16, name="b2_all")
         h_flat = h.rearrange("b s k -> b (s k)")
 
         def load_w1(half):
@@ -71,23 +69,24 @@ def tile_graphnetlayer_pa_kernel(tc, h, ew1, eb1, ew2, eb2, out):
 
         load_w1(0)
         nc.sync.dma_start(out=b1_rows[0:PACK, :], in_=eb1.rearrange("(t p) -> t p", p=P))
-        nc.sync.dma_start(out=b2_rows[0:1, :], in_=eb2.rearrange("(o n) -> o n", o=1))
         load_h(0)
         load_w1(1)
         load_h(1)
         nc.sync.dma_start(out=w2_raw[:], in_=ew2.rearrange("(t p) n -> p t n", p=P))
+        nc.sync.dma_start(out=b2_all[:], in_=eb2.partition_broadcast(P))
 
         ident_f32 = keep.tile([P, P], F32, name="ident_f32")
         ident_bf16 = keep.tile([P, P], BF16, name="ident_bf16")
         make_identity(nc, ident_f32[:])
         nc.vector.tensor_copy(out=ident_bf16[:], in_=ident_f32[:])
 
-        def regroup_weight(raw, grouped):
+        def regroup_weight(raw, grouped, vector_cols):
             src = raw.rearrange("p t (c i) -> p c t i", i=RUN)
             dst = grouped.rearrange("p (c i) t -> p c t i", i=RUN)
-            split = VECTOR_COLS // RUN
+            split = vector_cols // RUN
             nc.vector.tensor_copy(out=dst[:, :split], in_=src[:, :split])
-            nc.scalar.copy(out=dst[:, split:], in_=src[:, split:])
+            if vector_cols < raw.shape[2]:
+                nc.scalar.copy(out=dst[:, split:], in_=src[:, split:])
 
         def quantise(grouped, codes, scales):
             nc.vector.quantize_mx(
@@ -99,6 +98,10 @@ def tile_graphnetlayer_pa_kernel(tc, h, ew1, eb1, ew2, eb2, out):
         w1_grouped = keep.tile([P, 2, F, PACK], BF16, name="w1_grouped", align_bytes=64)
         w1_codes = keep.tile([P, 2, F], U32, name="w1_codes", align_bytes=64)
         w1_scales = keep.tile([P, 2, F], U8, name="w1_scales", align_bytes=64)
+
+        def quantise_w1(half, bank):
+            cols = slice(bank * BANK_F, (bank + 1) * BANK_F)
+            quantise(w1_grouped[:, half, cols], w1_codes[:, half, cols], w1_scales[:, half, cols])
 
         h_words = h_raw[:].bitcast(F32)
         h_grouped = keep.tile([P, NODES, P, PACK], BF16, name="h_grouped", align_bytes=64)
@@ -132,18 +135,25 @@ def tile_graphnetlayer_pa_kernel(tc, h, ew1, eb1, ew2, eb2, out):
                 h_scales[:, tokens],
             )
 
-        regroup_weight(w1_raw[:, 0], w1_grouped[:, 0])
+        regroup_weight(w1_raw[:, 0], w1_grouped[:, 0], VECTOR_COLS)
         b1_t = psum_node.tile([P, P], BF16, name="b1_t", tag="node_acc")
         nc.tensor.transpose(b1_t[:], b1_rows[:], ident_bf16[:])
         b1_col = keep.tile([P, PACK], F32, name="b1_col")
         nc.vector.tensor_copy(out=b1_col[:], in_=b1_t[:, 0:PACK])
-        quantise(w1_grouped[:, 0], w1_codes[:, 0], w1_scales[:, 0])
+        quantise_w1(0, 0)
+        quantise_w1(0, 1)
         flip_h(0)
-        regroup_weight(w1_raw[:, 1], w1_grouped[:, 1])
+        regroup_weight(w1_raw[:, 1], w1_grouped[:, 1], VECTOR_COLS)
         quantise_h(0)
-        quantise(w1_grouped[:, 1], w1_codes[:, 1], w1_scales[:, 1])
+        quantise_w1(1, 0)
+        quantise_w1(1, 1)
         flip_h(1)
+        w2_grouped = keep.tile([P, H, PACK], BF16, name="w2_grouped", align_bytes=64)
+        w2_codes = keep.tile([P, H], U32, name="w2_codes", align_bytes=64)
+        w2_scales = keep.tile([P, H], U8, name="w2_scales", align_bytes=64)
+        regroup_weight(w2_raw[:], w2_grouped[:], H)
         quantise_h(1)
+        quantise(w2_grouped[:], w2_codes[:], w2_scales[:])
 
         hidden_of = {}
         grouped_of = {}
@@ -241,23 +251,12 @@ def tile_graphnetlayer_pa_kernel(tc, h, ew1, eb1, ew2, eb2, out):
                 nc.sync.dma_start(out=out[:, node, :], in_=out_sb[:, node, :])
 
         layer1(0)
-        b2_sum = psum_node.tile([P, H], F32, name="b2_sum", tag="node_acc")
-        nc.tensor.matmul(b2_sum[:], lhsT=ones[:], rhs=b2_rows[:], start=True, stop=True)
-        b2_all = keep.tile([P, H], F32, name="b2_all")
-        nc.scalar.copy(out=b2_all[:], in_=b2_sum[:])
-        w2_grouped = keep.tile([P, H, PACK], BF16, name="w2_grouped", align_bytes=64)
-        w2_codes = keep.tile([P, H], U32, name="w2_codes", align_bytes=64)
-        w2_scales = keep.tile([P, H], U8, name="w2_scales", align_bytes=64)
-        regroup_weight(w2_raw[:], w2_grouped[:])
         regroup_hidden(0)
-        quantise(w2_grouped[:], w2_codes[:], w2_scales[:])
-        quantise_hidden(0)
         for u in range(1, len(units) + LAG):
             if u < len(units):
                 layer1(u)
-            finished = layer2(u - LAG) if u >= LAG else []
+            finish(layer2(u - LAG) if u >= LAG else [])
+            if u - 1 < len(units):
+                quantise_hidden(u - 1)
             if u < len(units):
                 regroup_hidden(u)
-            finish(finished)
-            if u < len(units):
-                quantise_hidden(u)

@@ -23,6 +23,8 @@ UNIT_EDGES = 2
 UNIT_TOKENS = UNIT_EDGES * P
 BANK_F = 2 * P
 LAG = 3
+WARM_HEAD = 10
+WARM_GAP = 4
 RUN = 4
 VECTOR_COLS = 352
 
@@ -48,6 +50,18 @@ def tile_graphnetlayer_pa_kernel(tc, h, ew1, eb1, ew2, eb2, out):
         stream = ctx.enter_context(tc.tile_pool(name="stream", bufs=LAG + 2))
         psum_hidden = ctx.enter_context(tc.psum_pool(name="psum_hidden", bufs=4))
         psum_node = ctx.enter_context(tc.psum_pool(name="psum_node", bufs=4))
+
+        warm_in = keep.tile([P, H], BF16, name="warm_in")
+        nc.vector.memset(warm_in[:], 0.0)
+        warm_out = psum_node.tile([P, H], F32, name="warm_out", tag="node_acc")
+
+        def keep_clock_up(matmuls):
+            for i in range(matmuls):
+                nc.tensor.matmul(
+                    warm_out[:], lhsT=warm_in[:, 0:P], rhs=warm_in[:], start=True, stop=True
+                )
+
+        keep_clock_up(WARM_HEAD)
 
         b1_rows = keep.tile([P, P], BF16, name="b1_rows")
         nc.vector.memset(b1_rows[:], 0.0)
@@ -147,6 +161,7 @@ def tile_graphnetlayer_pa_kernel(tc, h, ew1, eb1, ew2, eb2, out):
         quantise_h(0)
         quantise_w1(1, 0)
         quantise_w1(1, 1)
+        keep_clock_up(WARM_GAP)
         flip_h(1)
         w2_grouped = keep.tile([P, H, PACK], BF16, name="w2_grouped", align_bytes=64)
         w2_codes = keep.tile([P, H], U32, name="w2_codes", align_bytes=64)

from contextlib import ExitStack

import concourse.mybir as mybir
from concourse.masks import make_identity

BF16 = mybir.dt.bfloat16
F32 = mybir.dt.float32
U32 = mybir.dt.uint32
U8 = mybir.dt.uint8
FP8X4 = mybir.dt.float8_e4m3fn_x4
RELU = mybir.ActivationFunctionType.Relu
ADD = mybir.AluOpType.add
MULT = mybir.AluOpType.mult

P = 128
PACK = 4
NODES = 8
EDGES = NODES - 1
H = 512
F = 512
PART_NODES = 4
UNIT_EDGES = 2
UNIT_TOKENS = UNIT_EDGES * P
BANK_F = 2 * P
LAG = 3
WARM_HEAD = 10
WARM_GAP = 4
RUN = 4
VECTOR_COLS = 352

FLOPS = 2 * 2 * EDGES * P * (2 * H * F + F * H)


def edge_units():
    units = []
    for first in range(0, EDGES - 1, UNIT_EDGES):
        units.append([("rl", first, UNIT_EDGES)])
        units.append([("lr", first, UNIT_EDGES)])
    units.append([("rl", EDGES - 1, 1), ("lr", EDGES - 1, 1)])
    return units


def tile_graphnetlayer_pa_kernel(tc, h, ew1, eb1, ew2, eb2, out):
    nc = tc.nc
    units = edge_units()

    with ExitStack() as ctx:
        ctx.enter_context(tc.manual_schedule())
        keep = ctx.enter_context(tc.tile_pool(name="keep", bufs=1))
        stream = ctx.enter_context(tc.tile_pool(name="stream", bufs=LAG + 2))
        psum_hidden = ctx.enter_context(tc.psum_pool(name="psum_hidden", bufs=4))
        psum_node = ctx.enter_context(tc.psum_pool(name="psum_node", bufs=4))

        warm_in = keep.tile([P, H], BF16, name="warm_in")
        nc.vector.memset(warm_in[:], 0.0)
        warm_out = psum_node.tile([P, H], F32, name="warm_out", tag="node_acc")

        def keep_clock_up(matmuls):
            for i in range(matmuls):
                nc.tensor.matmul(
                    warm_out[:], lhsT=warm_in[:, 0:P], rhs=warm_in[:], start=True, stop=True
                )

        keep_clock_up(WARM_HEAD)

        b1_rows = keep.tile([P, P], BF16, name="b1_rows")
        nc.vector.memset(b1_rows[:], 0.0)
        w1_raw = keep.tile([P, 2, PACK, F], BF16, name="w1_raw")
        h_raw = keep.tile([P, NODES * H], BF16, name="h_raw")
        w2_raw = keep.tile([P, PACK, H], BF16, name="w2_raw")
        b2_all = keep.tile([P, H], BF16, name="b2_all")
        h_flat = h.rearrange("b s k -> b (s k)")

        def load_w1(half):
            nc.sync.dma_start(
                out=w1_raw[:, half].rearrange("p (u e) c -> p u e c", e=2),
                in_=ew1[half * H : (half + 1) * H, :].rearrange("(u p e) c -> p u e c", u=2, e=2),
            )

        def load_h(part):
            cols = slice(part * PART_NODES * H, (part + 1) * PART_NODES * H)
            nc.sync.dma_start(out=h_raw[:, cols], in_=h_flat[:, cols])

        load_w1(0)
        nc.sync.dma_start(out=b1_rows[0:PACK, :], in_=eb1.rearrange("(t p) -> t p", p=P))
        load_h(0)
        load_w1(1)
        load_h(1)
        nc.sync.dma_start(out=w2_raw[:], in_=ew2.rearrange("(t p) n -> p t n", p=P))
        nc.sync.dma_start(out=b2_all[:], in_=eb2.partition_broadcast(P))

        ident_f32 = keep.tile([P, P], F32, name="ident_f32")
        ident_bf16 = keep.tile([P, P], BF16, name="ident_bf16")
        make_identity(nc, ident_f32[:])
        nc.vector.tensor_copy(out=ident_bf16[:], in_=ident_f32[:])

        def regroup_weight(raw, grouped, vector_cols):
            src = raw.rearrange("p t (c i) -> p c t i", i=RUN)
            dst = grouped.rearrange("p (c i) t -> p c t i", i=RUN)
            split = vector_cols // RUN
            nc.vector.tensor_copy(out=dst[:, :split], in_=src[:, :split])
            if vector_cols < raw.shape[2]:
                nc.scalar.copy(out=dst[:, split:], in_=src[:, split:])

        def quantise(grouped, codes, scales):
            nc.vector.quantize_mx(
                out=codes.bitcast(FP8X4),
                scales=scales,
                in_=grouped.rearrange("p c t -> p (c t)"),
            )

        w1_grouped = keep.tile([P, 2, F, PACK], BF16, name="w1_grouped", align_bytes=64)
        w1_codes = keep.tile([P, 2, F], U32, name="w1_codes", align_bytes=64)
        w1_scales = keep.tile([P, 2, F], U8, name="w1_scales", align_bytes=64)

        def quantise_w1(half, bank):
            cols = slice(bank * BANK_F, (bank + 1) * BANK_F)
            quantise(w1_grouped[:, half, cols], w1_codes[:, half, cols], w1_scales[:, half, cols])

        h_words = h_raw[:].bitcast(F32)
        h_grouped = keep.tile([P, NODES, P, PACK], BF16, name="h_grouped", align_bytes=64)
        h_grouped_words = h_grouped[:].rearrange("p s b t -> p (s b t)").bitcast(F32)
        h_codes = keep.tile([P, NODES * P], U32, name="h_codes", align_bytes=64)
        h_scales = keep.tile([P, NODES * P], U8, name="h_scales", align_bytes=64)
        words = H // 2

        def flip_h(part):
            for pair in range(part * PART_NODES // 2, (part + 1) * PART_NODES // 2):
                flipped = psum_hidden.tile([P, 2, 2, P], F32, name="flipped", tag="hidden_acc")
                for s in range(2):
                    for u in range(2):
                        first = (2 * pair + s) * words + u * P
                        nc.tensor.transpose(
                            flipped[:, s, u, :], h_words[:, first : first + P], ident_f32[:]
                        )
                nc.scalar.copy(
                    out=h_grouped_words[:, 2 * pair * words : (2 * pair + 2) * words].rearrange(
                        "p (s b u) -> p s b u", s=2, u=2
                    ),
                    in_=flipped[:].rearrange("p s u b -> p s b u"),
                )

        def quantise_h(part):
            nodes = slice(part * PART_NODES, (part + 1) * PART_NODES)
            tokens = slice(part * PART_NODES * P, (part + 1) * PART_NODES * P)
            quantise(
                h_grouped[:, nodes].rearrange("p s b t -> p (s b) t"),
                h_codes[:, tokens],
                h_scales[:, tokens],
            )

        regroup_weight(w1_raw[:, 0], w1_grouped[:, 0], VECTOR_COLS)
        b1_t = psum_node.tile([P, P], BF16, name="b1_t", tag="node_acc")
        nc.tensor.transpose(b1_t[:], b1_rows[:], ident_bf16[:])
        b1_col = keep.tile([P, PACK], F32, name="b1_col")
        nc.vector.tensor_copy(out=b1_col[:], in_=b1_t[:, 0:PACK])
        quantise_w1(0, 0)
        quantise_w1(0, 1)
        flip_h(0)
        regroup_weight(w1_raw[:, 1], w1_grouped[:, 1], VECTOR_COLS)
        quantise_h(0)
        quantise_w1(1, 0)
        quantise_w1(1, 1)
        keep_clock_up(WARM_GAP)
        flip_h(1)
        w2_grouped = keep.tile([P, H, PACK], BF16, name="w2_grouped", align_bytes=64)
        w2_codes = keep.tile([P, H], U32, name="w2_codes", align_bytes=64)
        w2_scales = keep.tile([P, H], U8, name="w2_scales", align_bytes=64)
        regroup_weight(w2_raw[:], w2_grouped[:], H)
        quantise_h(1)
        quantise(w2_grouped[:], w2_codes[:], w2_scales[:])

        hidden_of = {}
        grouped_of = {}
        codes_of = {}
        node_acc = {}
        terms_seen = {}
        out_sb = keep.tile([P, NODES, H], F32, name="out_sb")

        def layer1(u):
            hidden = stream.tile([P, PACK, UNIT_TOKENS], BF16, name="hidden")
            hidden_of[u] = hidden
            for bank in range(PACK // 2):
                acc = psum_hidden.tile([P, 2, UNIT_TOKENS], F32, name="hidden_acc")
                for i in range(2):
                    f_cols = slice((2 * bank + i) * P, (2 * bank + i + 1) * P)
                    col = 0
                    for direction, first_edge, edges in units[u]:
                        width = edges * P
                        left = slice(first_edge * P, first_edge * P + width)
                        right = slice((first_edge + 1) * P, (first_edge + 1) * P + width)
                        joined = (left, right) if direction == "lr" else (right, left)
                        for half in range(2):
                            nc.tensor.matmul_mx(
                                out=acc[:, i, col : col + width],
                                lhsT=w1_codes[:, half, f_cols].bitcast(FP8X4),
                                lhsT_scale=w1_scales[:, half, f_cols],
                                rhs=h_codes[:, joined[half]].bitcast(FP8X4),
                                rhs_scale=h_scales[:, joined[half]],
                                start=(half == 0),
                                stop=(half == 1),
                            )
                        col += width
                for i in range(2):
                    t = 2 * bank + i
                    nc.scalar.activation(
                        out=hidden[:, t, :],
                        in_=acc[:, i, :],
                        func=RELU,
                        bias=b1_col[:, t : t + 1],
                        scale=1.0,
                    )

        def regroup_hidden(u):
            grouped = stream.tile([P, UNIT_TOKENS, PACK], BF16, name="grouped", align_bytes=64)
            grouped_of[u] = grouped
            nc.vector.tensor_copy(
                out=grouped.rearrange("p (c i) t -> p c t i", i=RUN),
                in_=hidden_of[u].rearrange("p t (c i) -> p c t i", i=RUN),
            )

        def quantise_hidden(u):
            codes = stream.tile([P, UNIT_TOKENS], U32, name="codes", align_bytes=64)
            scales = stream.tile([P, UNIT_TOKENS], U8, name="scales", align_bytes=64)
            codes_of[u] = (codes, scales)
            quantise(grouped_of[u], codes[:], scales[:])

        def layer2(u):
            codes, scales = codes_of[u]
            finished = []
            block = 0
            for direction, first_edge, edges in units[u]:
                for edge in range(first_edge, first_edge + edges):
                    node = edge + 1 if direction == "lr" else edge
                    terms = 1 if node in (0, NODES - 1) else 2
                    if node not in node_acc:
                        acc = psum_node.tile([P, H], F32, name="node_acc")
                        node_acc[node] = acc
                        terms_seen[node] = 0
                    terms_seen[node] += 1
                    tokens = slice(block * P, (block + 1) * P)
                    nc.tensor.matmul_mx(
                        out=node_acc[node][:],
                        lhsT=codes[:, tokens].bitcast(FP8X4),
                        lhsT_scale=scales[:, tokens],
                        rhs=w2_codes[:].bitcast(FP8X4),
                        rhs_scale=w2_scales[:],
                        start=(terms_seen[node] == 1),
                        stop=(terms_seen[node] == terms),
                    )
                    if terms_seen[node] == terms:
                        finished.append(node)
                    block += 1
            return finished

        def finish(nodes):
            for node in nodes:
                nc.vector.scalar_tensor_tensor(
                    out=out_sb[:, node, :],
                    in0=b2_all[:],
                    scalar=float(terms_seen[node]),
                    in1=node_acc[node][:],
                    op0=MULT,
                    op1=ADD,
                )
                nc.sync.dma_start(out=out[:, node, :], in_=out_sb[:, node, :])

        layer1(0)
        regroup_hidden(0)
        for u in range(1, len(units) + LAG):
            if u < len(units):
                layer1(u)
            finish(layer2(u - LAG) if u >= LAG else [])
            if u - 1 < len(units):
                quantise_hidden(u - 1)
            if u < len(units):
                regroup_hidden(u)
